import numpy as np
import ml_dtypes


def mxq(x, axis, fmt="e4m3"):
    dtype, down = {"e4m3": (ml_dtypes.float8_e4m3fn, 7), "e5m2": (ml_dtypes.float8_e5m2, 14)}[fmt]
    v = np.moveaxis(np.asarray(x, np.float32).astype(ml_dtypes.bfloat16).astype(np.float64), axis, -1)
    blocks = v.reshape(v.shape[:-1] + (-1, 32))
    amax = np.abs(blocks).max(-1, keepdims=True)
    byte = np.maximum(np.where(amax > 0, np.frexp(amax)[1] - 1 + 127, 0) - down, 1)
    scale = np.exp2(byte - 127.0)
    codes = (blocks / scale).astype(np.float32).astype(dtype).astype(np.float64)
    return np.moveaxis((codes * scale).reshape(v.shape), -1, axis)


WIDE = False


def mx_kscale(k):
    if not WIDE:
        return np.ones(k)
    levels = np.array([10, -10, 5, -5, 0])
    a = np.random.permutation(np.resize(levels, k // 512 * 4)).reshape(k // 512, 4)
    idx = np.arange(k)
    return np.exp2(a[idx // 512, idx % 128 // 32])


BF16 = ml_dtypes.bfloat16


def bf(x):
    return np.asarray(x, np.float32).astype(BF16)


def f64(x):
    return np.asarray(x).astype(np.float64)


B, D, T, N, H, DH = 4, 1024, 2048, 3, 2, 64
EPS = 1e-6
NEG_SLOPE = 0.2


def setup_inputs():
    s = mx_kscale(D)
    return {"x": bf(np.random.standard_normal((B, D, T)) * s[:, None]),
            "qkv": bf(np.random.standard_normal((N, H, D, DH)) * 1.4 / np.sqrt(D) / s[:, None]),
            "norm_w": bf(1.5 + 0.1 * np.random.standard_normal(1))}


def reference(x, qkv, norm_w):
    x = f64(x)
    a = np.where(x >= 0, x, NEG_SLOPE * x)
    aq = mxq(a, 1, "e4m3")
    wq = mxq(f64(qkv), 2, "e4m3")
    y = aq.transpose(0, 2, 1) @ wq.transpose(2, 0, 1, 3).reshape(D, N * H * DH)
    h = y.reshape(B, T, N, H, DH).transpose(2, 0, 3, 1, 4)
    denom = np.mean(h * h, axis=-2, keepdims=True)
    return f64(norm_w) * (h / np.sqrt(denom + EPS))

@@ -1,0 +1,168 @@
+from contextlib import ExitStack
+
+import concourse.mybir as mybir
+from concourse.masks import make_identity
+
+BF16 = mybir.dt.bfloat16
+F32 = mybir.dt.float32
+U32 = mybir.dt.uint32
+U8 = mybir.dt.uint8
+FP8X4 = mybir.dt.float8_e4m3fn_x4
+ACT = mybir.ActivationFunctionType
+ALU = mybir.AluOpType
+
+BATCH, CHANNELS, SEQ = 4, 1024, 2048
+N_QKV, HEADS, HEAD_DIM = 3, 2, 64
+NEG_SLOPE = 0.2
+EPS = 1e-6
+
+P = 128
+PACK = 4
+K_PASS = P * PACK
+PASSES = CHANNELS // K_PASS
+CHUNK = 512
+CHUNKS = SEQ // CHUNK
+RUN = CHUNK // P
+
+FLOPS = 2 * BATCH * SEQ * CHANNELS * N_QKV * HEADS * HEAD_DIM
+
+
+def tile_mha_pa_t_kernel(tc, x, qkv, norm_w, out):
+    nc = tc.nc
+    with ExitStack() as ctx:
+        const = ctx.enter_context(tc.tile_pool(name="const", bufs=1))
+        x_pool = ctx.enter_context(tc.tile_pool(name="x_pool", bufs=12))
+        grouped_pool = ctx.enter_context(tc.tile_pool(name="grouped_pool", bufs=3))
+        codes_pool = ctx.enter_context(tc.tile_pool(name="codes_pool", bufs=2))
+        stats_pool = ctx.enter_context(tc.tile_pool(name="stats_pool", bufs=2))
+        squares_pool = ctx.enter_context(tc.tile_pool(name="squares_pool", bufs=3))
+        scaled_pool = ctx.enter_context(tc.tile_pool(name="scaled_pool", bufs=3))
+        store_pool = ctx.enter_context(tc.tile_pool(name="store_pool", bufs=4))
+        psum_stats = ctx.enter_context(tc.psum_pool(name="psum_stats", bufs=2))
+        psum_scale = ctx.enter_context(tc.psum_pool(name="psum_scale", bufs=3))
+        psum_turned = ctx.enter_context(tc.psum_pool(name="psum_turned", bufs=3))
+
+        eps = const.tile([P, 1], F32)
+        nc.vector.memset(eps[:], EPS)
+        table_warmer = const.tile([P, 1], F32)
+        nc.scalar.activation(out=table_warmer[:], in_=eps[:], func=ACT.Sqrt)
+
+        identity = const.tile([P, P], F32)
+        make_identity(nc, identity[:])
+
+        gain_bf16 = const.tile([P, 1], BF16)
+        nc.scalar.dma_start(out=gain_bf16[:], in_=norm_w.partition_broadcast(P))
+        gain = const.tile([P, 1], F32)
+        nc.vector.tensor_copy(out=gain[:], in_=gain_bf16[:])
+
+        w_raw = const.tile([P, N_QKV, HEADS, PASSES, PACK, HEAD_DIM], BF16)
+        nc.scalar.dma_start(
+            out=w_raw[:],
+            in_=qkv.rearrange("n i (c p j) e -> p n i c j e", c=PASSES, p=P, j=PACK),
+        )
+        w_grouped = const.tile([P, N_QKV, PASSES, HEADS, HEAD_DIM, PACK], BF16, align_bytes=64)
+        w_codes = const.tile([P, N_QKV, PASSES, P], U32, align_bytes=64)
+        w_scales = const.tile([P, N_QKV, PASSES, P], U8, align_bytes=64)
+        for n in range(N_QKV):
+            for c in range(PASSES):
+                nc.scalar.copy(
+                    out=w_grouped[:, n, c],
+                    in_=w_raw[:, n, :, c].rearrange("p i j e -> p i e j"),
+                )
+        for n in range(N_QKV):
+            nc.vector.quantize_mx(
+                out=w_codes[:, n].rearrange("p c m -> p (c m)").bitcast(FP8X4),
+                scales=w_scales[:, n].rearrange("p c m -> p (c m)"),
+                in_=w_grouped[:, n].rearrange("p c i e j -> p (c i e j)"),
+            )
+
+        def project(psum_pool, a_codes, a_scales, n, q):
+            h = psum_pool.tile([P, CHUNK], F32)
+            for c in range(PASSES):
+                nc.tensor.matmul_mx(
+                    out=h[:],
+                    lhsT=w_codes[:, n, c, :].bitcast(FP8X4),
+                    lhsT_scale=w_scales[:, n, c, :],
+                    rhs=a_codes[:, q, c, :].bitcast(FP8X4),
+                    rhs_scale=a_scales[:, q, c, :],
+                    start=(c == 0),
+                    stop=(c == PASSES - 1),
+                )
+            return h
+
+        for b in range(BATCH):
+            a_codes = codes_pool.tile([P, CHUNKS, PASSES, CHUNK], U32, align_bytes=64)
+            a_scales = codes_pool.tile([P, CHUNKS, PASSES, CHUNK], U8, align_bytes=64)
+            sum_squares = stats_pool.tile([P, N_QKV, CHUNKS], F32)
+
+            for q in range(CHUNKS):
+                positions = slice(q * CHUNK, (q + 1) * CHUNK)
+                a_grouped = grouped_pool.tile([P, PASSES, CHUNK, PACK], BF16, align_bytes=64)
+                for c in range(PASSES):
+                    x_raw = x_pool.tile([P, PACK, CHUNK], BF16)
+                    nc.sync.dma_start(
+                        out=x_raw[:],
+                        in_=x[b, c * K_PASS : (c + 1) * K_PASS, positions].rearrange(
+                            "(p j) t -> p j t", j=PACK
+                        ),
+                    )
+                    x_by_position = x_raw[:].rearrange("p j t -> p t j")
+                    nc.vector.scalar_tensor_tensor(
+                        out=a_grouped[:, c],
+                        in0=x_by_position,
+                        scalar=NEG_SLOPE,
+                        in1=x_by_position,
+                        op0=ALU.mult,
+                        op1=ALU.max,
+                    )
+                nc.vector.quantize_mx(
+                    out=a_codes[:, q].rearrange("p c t -> p (c t)").bitcast(FP8X4),
+                    scales=a_scales[:, q].rearrange("p c t -> p (c t)"),
+                    in_=a_grouped[:].rearrange("p c t j -> p (c t j)"),
+                )
+                for n in range(N_QKV):
+                    h = project(psum_stats, a_codes, a_scales, n, q)
+                    squares = squares_pool.tile([P, CHUNK], BF16)
+                    nc.scalar.activation(
+                        out=squares[:],
+                        in_=h[:],
+                        func=ACT.Square,
+                        accum_out=sum_squares[:, n, q : q + 1],
+                    )
+
+            total = stats_pool.tile([P, N_QKV], F32)
+            nc.vector.tensor_reduce(
+                out=total[:], in_=sum_squares[:], axis=mybir.AxisListType.X, op=ALU.add
+            )
+            rms = stats_pool.tile([P, N_QKV], F32)
+            nc.scalar.activation(
+                out=rms[:], in_=total[:], func=ACT.Sqrt, scale=1.0 / SEQ, bias=eps[:, 0:1]
+            )
+            inverse_rms = stats_pool.tile([P, N_QKV], F32)
+            nc.vector.reciprocal(out=inverse_rms[:], in_=rms[:])
+            factor = stats_pool.tile([P, N_QKV], F32)
+            nc.vector.tensor_scalar_mul(out=factor[:], in0=inverse_rms[:], scalar1=gain[:, 0:1])
+
+            for n in range(N_QKV):
+                for q in range(CHUNKS):
+                    positions = slice(q * CHUNK, (q + 1) * CHUNK)
+                    h = project(psum_scale, a_codes, a_scales, n, q)
+                    h_scaled = scaled_pool.tile([P, RUN, P], F32)
+                    nc.scalar.activation(
+                        out=h_scaled[:],
+                        in_=h[:].rearrange("m (r s) -> m s r", s=RUN),
+                        func=ACT.Copy,
+                        scale=factor[:, n : n + 1],
+                    )
+                    turned = psum_turned.tile([P, RUN, P], F32)
+                    for s in range(RUN):
+                        nc.tensor.transpose(turned[:, s, :], h_scaled[:, s, :], identity[:])
+                    to_store = store_pool.tile([P, HEADS, RUN, HEAD_DIM], F32)
+                    nc.scalar.copy(
+                        out=to_store[:],
+                        in_=turned[:].rearrange("r s (i e) -> r i s e", i=HEADS),
+                    )
+                    nc.sync.dma_start(
+                        out=out[n, b, :, positions, :].rearrange("i (r s) e -> r i (s e)", s=RUN),
+                        in_=to_store[:].rearrange("r i s e -> r i (s e)"),
+                    )

@@ -149,8 +149,8 @@ def tile_mha_pa_t_kernel(tc, x, qkv, norm_w, out):
                     h = project(psum_scale, a_codes, a_scales, n, q)
                     h_scaled = scaled_pool.tile([P, RUN, P], F32)
                     nc.scalar.activation(
-                        out=h_scaled[:],
-                        in_=h[:].rearrange("m (r s) -> m s r", s=RUN),
+                        out=h_scaled[:].rearrange("m s r -> m r s"),
+                        in_=h[:].rearrange("m (r s) -> m r s", s=RUN),
                         func=ACT.Copy,
                         scale=factor[:, n : n + 1],
                     )

@@ -24,6 +24,12 @@ CHUNK = 512
 CHUNKS = SEQ // CHUNK
 RUN = CHUNK // P
 
+ALL_CHUNKS = BATCH * CHUNKS
+HALVES = ALL_CHUNKS * PASSES
+LOADS_AHEAD = 8
+SCALE_LAG = CHUNKS
+STORE_LAG = SCALE_LAG + 1
+
 FLOPS = 2 * BATCH * SEQ * CHANNELS * N_QKV * HEADS * HEAD_DIM
 
 
@@ -31,53 +37,67 @@ def tile_mha_pa_t_kernel(tc, x, qkv, norm_w, out):
     nc = tc.nc
     with ExitStack() as ctx:
         const = ctx.enter_context(tc.tile_pool(name="const", bufs=1))
-        x_pool = ctx.enter_context(tc.tile_pool(name="x_pool", bufs=12))
+        x_pool = ctx.enter_context(tc.tile_pool(name="x_pool", bufs=LOADS_AHEAD))
         grouped_pool = ctx.enter_context(tc.tile_pool(name="grouped_pool", bufs=3))
-        codes_pool = ctx.enter_context(tc.tile_pool(name="codes_pool", bufs=2))
+        codes_pool = ctx.enter_context(tc.tile_pool(name="codes_pool", bufs=3))
         stats_pool = ctx.enter_context(tc.tile_pool(name="stats_pool", bufs=2))
         squares_pool = ctx.enter_context(tc.tile_pool(name="squares_pool", bufs=3))
-        scaled_pool = ctx.enter_context(tc.tile_pool(name="scaled_pool", bufs=3))
-        store_pool = ctx.enter_context(tc.tile_pool(name="store_pool", bufs=4))
-        psum_stats = ctx.enter_context(tc.psum_pool(name="psum_stats", bufs=2))
-        psum_scale = ctx.enter_context(tc.psum_pool(name="psum_scale", bufs=3))
+        scaled_pool = ctx.enter_context(tc.tile_pool(name="scaled_pool", bufs=2 * N_QKV + 2))
+        store_pool = ctx.enter_context(tc.tile_pool(name="store_pool", bufs=2 * N_QKV))
+        psum_products = ctx.enter_context(tc.psum_pool(name="psum_products", bufs=5))
         psum_turned = ctx.enter_context(tc.psum_pool(name="psum_turned", bufs=3))
+        ctx.enter_context(tc.manual_schedule())
 
-        eps = const.tile([P, 1], F32)
-        nc.vector.memset(eps[:], EPS)
-        table_warmer = const.tile([P, 1], F32)
-        nc.scalar.activation(out=table_warmer[:], in_=eps[:], func=ACT.Sqrt)
+        x_tiles = {}
+        grouped_tiles = {}
+        code_tiles = {}
+        sum_tiles = {}
+        factor_tiles = {}
+        scaled_tiles = {}
 
-        identity = const.tile([P, P], F32)
-        make_identity(nc, identity[:])
+        def load_half(half):
+            chunk, c = divmod(half, PASSES)
+            b, q = divmod(chunk, CHUNKS)
+            x_raw = x_pool.tile([P, PACK, CHUNK], BF16)
+            nc.sync.dma_start(
+                out=x_raw[:],
+                in_=x[
+                    b, c * K_PASS : (c + 1) * K_PASS, q * CHUNK : (q + 1) * CHUNK
+                ].rearrange("(p j) t -> p j t", j=PACK),
+            )
+            x_tiles[half] = x_raw
 
-        gain_bf16 = const.tile([P, 1], BF16)
-        nc.scalar.dma_start(out=gain_bf16[:], in_=norm_w.partition_broadcast(P))
-        gain = const.tile([P, 1], F32)
-        nc.vector.tensor_copy(out=gain[:], in_=gain_bf16[:])
+        def leaky_relu_half(half):
+            a_grouped = grouped_pool.tile([P, CHUNK, PACK], BF16, align_bytes=64)
+            x_by_position = x_tiles[half][:].rearrange("p j t -> p t j")
+            nc.vector.scalar_tensor_tensor(
+                out=a_grouped[:],
+                in0=x_by_position,
+                scalar=NEG_SLOPE,
+                in1=x_by_position,
+                op0=ALU.mult,
+                op1=ALU.max,
+            )
+            grouped_tiles[half] = a_grouped
 
-        w_raw = const.tile([P, N_QKV, HEADS, PASSES, PACK, HEAD_DIM], BF16)
-        nc.scalar.dma_start(
-            out=w_raw[:],
-            in_=qkv.rearrange("n i (c p j) e -> p n i c j e", c=PASSES, p=P, j=PACK),
-        )
-        w_grouped = const.tile([P, N_QKV, PASSES, HEADS, HEAD_DIM, PACK], BF16, align_bytes=64)
-        w_codes = const.tile([P, N_QKV, PASSES, P], U32, align_bytes=64)
-        w_scales = const.tile([P, N_QKV, PASSES, P], U8, align_bytes=64)
-        for n in range(N_QKV):
-            for c in range(PASSES):
-                nc.scalar.copy(
-                    out=w_grouped[:, n, c],
-                    in_=w_raw[:, n, :, c].rearrange("p i j e -> p i e j"),
-                )
-        for n in range(N_QKV):
+        def quantise_half(half):
+            chunk, c = divmod(half, PASSES)
+            b, q = divmod(chunk, CHUNKS)
+            if b not in code_tiles:
+                a_codes = codes_pool.tile([P, CHUNKS, PASSES, CHUNK], U32, align_bytes=64)
+                a_scales = codes_pool.tile([P, CHUNKS, PASSES, CHUNK], U8, align_bytes=64)
+                code_tiles[b] = (a_codes, a_scales)
+            a_codes, a_scales = code_tiles[b]
             nc.vector.quantize_mx(
-                out=w_codes[:, n].rearrange("p c m -> p (c m)").bitcast(FP8X4),
-                scales=w_scales[:, n].rearrange("p c m -> p (c m)"),
-                in_=w_grouped[:, n].rearrange("p c i e j -> p (c i e j)"),
+                out=a_codes[:, q, c, :].bitcast(FP8X4),
+                scales=a_scales[:, q, c, :],
+                in_=grouped_tiles[half][:].rearrange("p t j -> p (t j)"),
             )
 
-        def project(psum_pool, a_codes, a_scales, n, q):
-            h = psum_pool.tile([P, CHUNK], F32)
+        def project(chunk, n):
+            b, q = divmod(chunk, CHUNKS)
+            a_codes, a_scales = code_tiles[b]
+            h = psum_products.tile([P, CHUNK], F32)
             for c in range(PASSES):
                 nc.tensor.matmul_mx(
                     out=h[:],
@@ -90,79 +110,137 @@ def tile_mha_pa_t_kernel(tc, x, qkv, norm_w, out):
                 )
             return h
 
-        for b in range(BATCH):
-            a_codes = codes_pool.tile([P, CHUNKS, PASSES, CHUNK], U32, align_bytes=64)
-            a_scales = codes_pool.tile([P, CHUNKS, PASSES, CHUNK], U8, align_bytes=64)
-            sum_squares = stats_pool.tile([P, N_QKV, CHUNKS], F32)
-
-            for q in range(CHUNKS):
-                positions = slice(q * CHUNK, (q + 1) * CHUNK)
-                a_grouped = grouped_pool.tile([P, PASSES, CHUNK, PACK], BF16, align_bytes=64)
-                for c in range(PASSES):
-                    x_raw = x_pool.tile([P, PACK, CHUNK], BF16)
-                    nc.sync.dma_start(
-                        out=x_raw[:],
-                        in_=x[b, c * K_PASS : (c + 1) * K_PASS, positions].rearrange(
-                            "(p j) t -> p j t", j=PACK
-                        ),
-                    )
-                    x_by_position = x_raw[:].rearrange("p j t -> p t j")
-                    nc.vector.scalar_tensor_tensor(
-                        out=a_grouped[:, c],
-                        in0=x_by_position,
-                        scalar=NEG_SLOPE,
-                        in1=x_by_position,
-                        op0=ALU.mult,
-                        op1=ALU.max,
-                    )
-                nc.vector.quantize_mx(
-                    out=a_codes[:, q].rearrange("p c t -> p (c t)").bitcast(FP8X4),
-                    scales=a_scales[:, q].rearrange("p c t -> p (c t)"),
-                    in_=a_grouped[:].rearrange("p c t j -> p (c t j)"),
-                )
-                for n in range(N_QKV):
-                    h = project(psum_stats, a_codes, a_scales, n, q)
-                    squares = squares_pool.tile([P, CHUNK], BF16)
-                    nc.scalar.activation(
-                        out=squares[:],
-                        in_=h[:],
-                        func=ACT.Square,
-                        accum_out=sum_squares[:, n, q : q + 1],
-                    )
-
-            total = stats_pool.tile([P, N_QKV], F32)
-            nc.vector.tensor_reduce(
-                out=total[:], in_=sum_squares[:], axis=mybir.AxisListType.X, op=ALU.add
-            )
-            rms = stats_pool.tile([P, N_QKV], F32)
-            nc.scalar.activation(
-                out=rms[:], in_=total[:], func=ACT.Sqrt, scale=1.0 / SEQ, bias=eps[:, 0:1]
-            )
-            inverse_rms = stats_pool.tile([P, N_QKV], F32)
-            nc.vector.reciprocal(out=inverse_rms[:], in_=rms[:])
-            factor = stats_pool.tile([P, N_QKV], F32)
-            nc.vector.tensor_scalar_mul(out=factor[:], in0=inverse_rms[:], scalar1=gain[:, 0:1])
-
+        def sum_squares_of_chunk(chunk):
+            b, q = divmod(chunk, CHUNKS)
+            if q == 0:
+                sum_squares = stats_pool.tile([P, N_QKV, CHUNKS], F32)
+                sum_tiles[b] = sum_squares
             for n in range(N_QKV):
-                for q in range(CHUNKS):
-                    positions = slice(q * CHUNK, (q + 1) * CHUNK)
-                    h = project(psum_scale, a_codes, a_scales, n, q)
-                    h_scaled = scaled_pool.tile([P, RUN, P], F32)
+                h = project(chunk, n)
+                squares = squares_pool.tile([P, CHUNK], BF16)
+                nc.scalar.activation(
+                    out=squares[:],
+                    in_=h[:],
+                    func=ACT.Square,
+                    accum_out=sum_tiles[b][:, n, q : q + 1],
+                )
+
+        def norm_factor_of_batch(b):
+            total = stats_pool.tile([P, N_QKV], F32)
+            copied = stats_pool.tile([P, N_QKV, CHUNKS], F32)
+            for n in range(N_QKV):
+                nc.scalar.activation(
+                    out=copied[:, n, :],
+                    in_=sum_tiles[b][:, n, :],
+                    func=ACT.Copy,
+                    accum_out=total[:, n : n + 1],
+                )
+            inverse_rms = stats_pool.tile([P, N_QKV], F32)
+            nc.scalar.activation(
+                out=inverse_rms[:],
+                in_=total[:],
+                func=ACT.Abs_reciprocal_sqrt,
+                scale=1.0 / SEQ,
+                bias=eps[:, 0:1],
+            )
+            factor = stats_pool.tile([P, N_QKV], F32)
+            nc.scalar.activation(
+                out=factor[:], in_=inverse_rms[:], func=ACT.Copy, scale=gain[:, 0:1]
+            )
+            factor_tiles[b] = factor
+
+        def scale_chunk(chunk, vector_is_free):
+            b = chunk // CHUNKS
+            for n in range(N_QKV):
+                h = project(chunk, n)
+                h_by_block = h[:].rearrange("m (r s) -> m s r", s=RUN)
+                h_scaled = scaled_pool.tile([P, RUN, P], F32)
+                if vector_is_free:
+                    nc.vector.tensor_scalar_mul(
+                        out=h_scaled[:], in0=h_by_block, scalar1=factor_tiles[b][:, n : n + 1]
+                    )
+                else:
                     nc.scalar.activation(
-                        out=h_scaled[:].rearrange("m s r -> m r s"),
-                        in_=h[:].rearrange("m (r s) -> m r s", s=RUN),
+                        out=h_scaled[:],
+                        in_=h_by_block,
                         func=ACT.Copy,
-                        scale=factor[:, n : n + 1],
+                        scale=factor_tiles[b][:, n : n + 1],
                     )
-                    turned = psum_turned.tile([P, RUN, P], F32)
-                    for s in range(RUN):
-                        nc.tensor.transpose(turned[:, s, :], h_scaled[:, s, :], identity[:])
-                    to_store = store_pool.tile([P, HEADS, RUN, HEAD_DIM], F32)
-                    nc.scalar.copy(
-                        out=to_store[:],
-                        in_=turned[:].rearrange("r s (i e) -> r i s e", i=HEADS),
-                    )
-                    nc.sync.dma_start(
-                        out=out[n, b, :, positions, :].rearrange("i (r s) e -> r i (s e)", s=RUN),
-                        in_=to_store[:].rearrange("r i s e -> r i (s e)"),
-                    )
+                scaled_tiles[(chunk, n)] = h_scaled
+
+        def store_chunk(chunk):
+            b, q = divmod(chunk, CHUNKS)
+            for n in range(N_QKV):
+                h_scaled = scaled_tiles[(chunk, n)]
+                turned = psum_turned.tile([P, RUN, P], F32)
+                for s in range(RUN):
+                    nc.tensor.transpose(turned[:, s, :], h_scaled[:, s, :], identity[:])
+                to_store = store_pool.tile([P, HEADS, RUN, HEAD_DIM], F32)
+                nc.scalar.copy(
+                    out=to_store[:], in_=turned[:].rearrange("r s (i e) -> r i s e", i=HEADS)
+                )
+                nc.sync.dma_start(
+                    out=out[n, b, :, q * CHUNK : (q + 1) * CHUNK, :].rearrange(
+                        "i (r s) e -> r i (s e)", s=RUN
+                    ),
+                    in_=to_store[:].rearrange("r i s e -> r i (s e)"),
+                )
+
+        load_half(0)
+        load_half(1)
+        w_raw = const.tile([P, N_QKV, HEADS, PASSES, PACK, HEAD_DIM], BF16)
+        nc.scalar.dma_start(
+            out=w_raw[:],
+            in_=qkv.rearrange("n i (c p j) e -> p n i c j e", c=PASSES, p=P, j=PACK),
+        )
+        gain_bf16 = const.tile([P, 1], BF16)
+        nc.scalar.dma_start(out=gain_bf16[:], in_=norm_w.partition_broadcast(P))
+        for half in range(2, LOADS_AHEAD):
+            load_half(half)
+
+        eps = const.tile([P, 1], F32)
+        nc.vector.memset(eps[:], EPS)
+        table_warmer = const.tile([P, 1], F32)
+        nc.scalar.activation(out=table_warmer[:], in_=eps[:], func=ACT.Abs_reciprocal_sqrt)
+        identity = const.tile([P, P], F32)
+        make_identity(nc, identity[:])
+        gain = const.tile([P, 1], F32)
+        nc.scalar.copy(out=gain[:], in_=gain_bf16[:])
+
+        w_grouped = const.tile([P, N_QKV, PASSES, HEADS, HEAD_DIM, PACK], BF16, align_bytes=64)
+        w_codes = const.tile([P, N_QKV, PASSES, P], U32, align_bytes=64)
+        w_scales = const.tile([P, N_QKV, PASSES, P], U8, align_bytes=64)
+        for n in range(N_QKV):
+            for c in range(PASSES):
+                nc.scalar.copy(
+                    out=w_grouped[:, n, c],
+                    in_=w_raw[:, n, :, c].rearrange("p i j e -> p i e j"),
+                )
+
+        def quantise_weights():
+            for n in range(N_QKV):
+                nc.vector.quantize_mx(
+                    out=w_codes[:, n].rearrange("p c m -> p (c m)").bitcast(FP8X4),
+                    scales=w_scales[:, n].rearrange("p c m -> p (c m)"),
+                    in_=w_grouped[:, n].rearrange("p c i e j -> p (c i e j)"),
+                )
+
+        for step in range(ALL_CHUNKS + STORE_LAG):
+            for half in range(PASSES * step, PASSES * (step + 1)):
+                if half < HALVES:
+                    leaky_relu_half(half)
+                    if half + LOADS_AHEAD < HALVES:
+                        load_half(half + LOADS_AHEAD)
+                if 1 <= half <= HALVES:
+                    quantise_half(half - 1)
+                if half == PASSES:
+                    quantise_weights()
+
+            if 0 <= step - 1 < ALL_CHUNKS:
+                sum_squares_of_chunk(step - 1)
+                if step % CHUNKS == 0:
+                    norm_factor_of_batch(step // CHUNKS - 1)
+            if 0 <= step - SCALE_LAG < ALL_CHUNKS:
+                scale_chunk(step - SCALE_LAG, vector_is_free=(step >= ALL_CHUNKS))
+            if 0 <= step - STORE_LAG < ALL_CHUNKS:
+                store_chunk(step - STORE_LAG)

@@ -29,6 +29,7 @@ HALVES = ALL_CHUNKS * PASSES
 LOADS_AHEAD = 8
 SCALE_LAG = CHUNKS
 STORE_LAG = SCALE_LAG + 1
+VECTOR_SHARE = 1
 
 FLOPS = 2 * BATCH * SEQ * CHANNELS * N_QKV * HEADS * HEAD_DIM
 
@@ -155,7 +156,7 @@ def tile_mha_pa_t_kernel(tc, x, qkv, norm_w, out):
                 h = project(chunk, n)
                 h_by_block = h[:].rearrange("m (r s) -> m s r", s=RUN)
                 h_scaled = scaled_pool.tile([P, RUN, P], F32)
-                if vector_is_free:
+                if vector_is_free or n < VECTOR_SHARE:
                     nc.vector.tensor_scalar_mul(
                         out=h_scaled[:], in0=h_by_block, scalar1=factor_tiles[b][:, n : n + 1]
                     )

@@ -29,7 +29,10 @@ HALVES = ALL_CHUNKS * PASSES
 LOADS_AHEAD = 8
 SCALE_LAG = CHUNKS
 STORE_LAG = SCALE_LAG + 1
-VECTOR_SHARE = 1
+FIRST_HELPED = 3
+LAST_HELPED = 10
+HELP_AHEAD = 4
+LINE_RUN = 4
 
 FLOPS = 2 * BATCH * SEQ * CHANNELS * N_QKV * HEADS * HEAD_DIM
 
@@ -40,6 +43,8 @@ def tile_mha_pa_t_kernel(tc, x, qkv, norm_w, out):
         const = ctx.enter_context(tc.tile_pool(name="const", bufs=1))
         x_pool = ctx.enter_context(tc.tile_pool(name="x_pool", bufs=LOADS_AHEAD))
         grouped_pool = ctx.enter_context(tc.tile_pool(name="grouped_pool", bufs=3))
+        helped_pool = ctx.enter_context(tc.tile_pool(name="helped_pool", bufs=HELP_AHEAD + 2))
+        fifth_pool = ctx.enter_context(tc.tile_pool(name="fifth_pool", bufs=2))
         codes_pool = ctx.enter_context(tc.tile_pool(name="codes_pool", bufs=3))
         stats_pool = ctx.enter_context(tc.tile_pool(name="stats_pool", bufs=2))
         squares_pool = ctx.enter_context(tc.tile_pool(name="squares_pool", bufs=3))
@@ -50,6 +55,8 @@ def tile_mha_pa_t_kernel(tc, x, qkv, norm_w, out):
         ctx.enter_context(tc.manual_schedule())
 
         x_tiles = {}
+        regrouped_tiles = {}
+        fifth_tiles = {}
         grouped_tiles = {}
         code_tiles = {}
         sum_tiles = {}
@@ -68,18 +75,48 @@ def tile_mha_pa_t_kernel(tc, x, qkv, norm_w, out):
             )
             x_tiles[half] = x_raw
 
-        def leaky_relu_half(half):
-            a_grouped = grouped_pool.tile([P, CHUNK, PACK], BF16, align_bytes=64)
-            x_by_position = x_tiles[half][:].rearrange("p j t -> p t j")
-            nc.vector.scalar_tensor_tensor(
-                out=a_grouped[:],
-                in0=x_by_position,
-                scalar=NEG_SLOPE,
-                in1=x_by_position,
-                op0=ALU.mult,
-                op1=ALU.max,
+        def scalar_helps(half):
+            return FIRST_HELPED <= half <= LAST_HELPED
+
+        def regroup_half_on_scalar(half):
+            x_grouped = helped_pool.tile([P, CHUNK, PACK], BF16)
+            nc.scalar.copy(
+                out=x_grouped[:].rearrange("p (g i) j -> p g j i", i=LINE_RUN),
+                in_=x_tiles[half][:].rearrange("p j (g i) -> p g j i", i=LINE_RUN),
             )
-            grouped_tiles[half] = a_grouped
+            regrouped_tiles[half] = x_grouped
+
+        def begin_leaky_relu(half):
+            if scalar_helps(half):
+                fifth = fifth_pool.tile([P, CHUNK * PACK], BF16)
+                nc.vector.tensor_scalar_mul(
+                    out=fifth[:],
+                    in0=regrouped_tiles[half][:].rearrange("p t j -> p (t j)"),
+                    scalar1=NEG_SLOPE,
+                )
+                fifth_tiles[half] = fifth
+            else:
+                a_grouped = grouped_pool.tile([P, CHUNK * PACK], BF16, align_bytes=64)
+                x_by_position = x_tiles[half][:].rearrange("p j t -> p t j")
+                nc.vector.scalar_tensor_tensor(
+                    out=a_grouped[:].rearrange("p (t j) -> p t j", j=PACK),
+                    in0=x_by_position,
+                    scalar=NEG_SLOPE,
+                    in1=x_by_position,
+                    op0=ALU.mult,
+                    op1=ALU.max,
+                )
+                grouped_tiles[half] = a_grouped
+
+        def end_leaky_relu(half):
+            if scalar_helps(half):
+                a_grouped = grouped_pool.tile([P, CHUNK * PACK], BF16, align_bytes=64)
+                nc.vector.tensor_max(
+                    out=a_grouped[:],
+                    in0=regrouped_tiles[half][:].rearrange("p t j -> p (t j)"),
+                    in1=fifth_tiles[half][:],
+                )
+                grouped_tiles[half] = a_grouped
 
         def quantise_half(half):
             chunk, c = divmod(half, PASSES)
@@ -92,7 +129,7 @@ def tile_mha_pa_t_kernel(tc, x, qkv, norm_w, out):
             nc.vector.quantize_mx(
                 out=a_codes[:, q, c, :].bitcast(FP8X4),
                 scales=a_scales[:, q, c, :],
-                in_=grouped_tiles[half][:].rearrange("p t j -> p (t j)"),
+                in_=grouped_tiles[half][:],
             )
 
         def project(chunk, n):
@@ -156,7 +193,7 @@ def tile_mha_pa_t_kernel(tc, x, qkv, norm_w, out):
                 h = project(chunk, n)
                 h_by_block = h[:].rearrange("m (r s) -> m s r", s=RUN)
                 h_scaled = scaled_pool.tile([P, RUN, P], F32)
-                if vector_is_free or n < VECTOR_SHARE:
+                if vector_is_free:
                     nc.vector.tensor_scalar_mul(
                         out=h_scaled[:], in0=h_by_block, scalar1=factor_tiles[b][:, n : n + 1]
                     )
@@ -226,14 +263,22 @@ def tile_mha_pa_t_kernel(tc, x, qkv, norm_w, out):
                     in_=w_grouped[:, n].rearrange("p c i e j -> p (c i e j)"),
                 )
 
+        for half in range(HELP_AHEAD):
+            if scalar_helps(half):
+                regroup_half_on_scalar(half)
+
         for step in range(ALL_CHUNKS + STORE_LAG):
             for half in range(PASSES * step, PASSES * (step + 1)):
+                if scalar_helps(half + HELP_AHEAD):
+                    regroup_half_on_scalar(half + HELP_AHEAD)
                 if half < HALVES:
-                    leaky_relu_half(half)
+                    begin_leaky_relu(half)
                     if half + LOADS_AHEAD < HALVES:
                         load_half(half + LOADS_AHEAD)
                 if 1 <= half <= HALVES:
                     quantise_half(half - 1)
+                if half < HALVES:
+                    end_leaky_relu(half)
                 if half == PASSES:
                     quantise_weights()
 

@@ -30,7 +30,8 @@ LOADS_AHEAD = 8
 SCALE_LAG = CHUNKS
 STORE_LAG = SCALE_LAG + 1
 FIRST_HELPED = 3
-LAST_HELPED = 10
+LAST_HELPED = 8
+HELP_PERIOD = 4
 HELP_AHEAD = 4
 LINE_RUN = 4
 
@@ -76,7 +77,9 @@ def tile_mha_pa_t_kernel(tc, x, qkv, norm_w, out):
             x_tiles[half] = x_raw
 
         def scalar_helps(half):
-            return FIRST_HELPED <= half <= LAST_HELPED
+            if FIRST_HELPED <= half <= LAST_HELPED:
+                return True
+            return LAST_HELPED < half < HALVES and (half - LAST_HELPED) % HELP_PERIOD == 0
 
         def regroup_half_on_scalar(half):
             x_grouped = helped_pool.tile([P, CHUNK, PACK], BF16)

@@ -156,6 +156,7 @@ def tile_mha_pa_t_kernel(tc, x, qkv, norm_w, out):
             if q == 0:
                 sum_squares = stats_pool.tile([P, N_QKV, CHUNKS], F32)
                 sum_tiles[b] = sum_squares
+            products = []
             for n in range(N_QKV):
                 h = project(chunk, n)
                 squares = squares_pool.tile([P, CHUNK], BF16)
@@ -165,6 +166,8 @@ def tile_mha_pa_t_kernel(tc, x, qkv, norm_w, out):
                     func=ACT.Square,
                     accum_out=sum_tiles[b][:, n, q : q + 1],
                 )
+                products.append(h)
+            return products
 
         def norm_factor_of_batch(b):
             total = stats_pool.tile([P, N_QKV], F32)
@@ -190,10 +193,10 @@ def tile_mha_pa_t_kernel(tc, x, qkv, norm_w, out):
             )
             factor_tiles[b] = factor
 
-        def scale_chunk(chunk, vector_is_free):
+        def scale_chunk(chunk, vector_is_free, products=None):
             b = chunk // CHUNKS
             for n in range(N_QKV):
-                h = project(chunk, n)
+                h = products[n] if products else project(chunk, n)
                 h_by_block = h[:].rearrange("m (r s) -> m s r", s=RUN)
                 h_scaled = scaled_pool.tile([P, RUN, P], F32)
                 if vector_is_free:
@@ -270,26 +273,39 @@ def tile_mha_pa_t_kernel(tc, x, qkv, norm_w, out):
             if scalar_helps(half):
                 regroup_half_on_scalar(half)
 
-        for step in range(ALL_CHUNKS + STORE_LAG):
+        for step in range(ALL_CHUNKS):
             for half in range(PASSES * step, PASSES * (step + 1)):
                 if scalar_helps(half + HELP_AHEAD):
                     regroup_half_on_scalar(half + HELP_AHEAD)
-                if half < HALVES:
-                    begin_leaky_relu(half)
-                    if half + LOADS_AHEAD < HALVES:
-                        load_half(half + LOADS_AHEAD)
-                if 1 <= half <= HALVES:
+                begin_leaky_relu(half)
+                if half + LOADS_AHEAD < HALVES:
+                    load_half(half + LOADS_AHEAD)
+                if half >= 1:
                     quantise_half(half - 1)
-                if half < HALVES:
-                    end_leaky_relu(half)
+                end_leaky_relu(half)
                 if half == PASSES:
                     quantise_weights()
+            vector_is_free = step == ALL_CHUNKS - 1
+            if vector_is_free:
+                quantise_half(HALVES - 1)
 
-            if 0 <= step - 1 < ALL_CHUNKS:
+            if step >= 1:
                 sum_squares_of_chunk(step - 1)
                 if step % CHUNKS == 0:
                     norm_factor_of_batch(step // CHUNKS - 1)
-            if 0 <= step - SCALE_LAG < ALL_CHUNKS:
-                scale_chunk(step - SCALE_LAG, vector_is_free=(step >= ALL_CHUNKS))
-            if 0 <= step - STORE_LAG < ALL_CHUNKS:
+            if step >= SCALE_LAG:
+                scale_chunk(step - SCALE_LAG, vector_is_free)
+            if step >= STORE_LAG:
                 store_chunk(step - STORE_LAG)
+
+        last = ALL_CHUNKS - 1
+        last_products = sum_squares_of_chunk(last)
+        norm_factor_of_batch(BATCH - 1)
+        store_chunk(last - SCALE_LAG)
+        scale_chunk(last, True, last_products)
+        scaled_before = last
+        for chunk in range(last - CHUNKS + 1, last):
+            scale_chunk(chunk, True)
+            store_chunk(scaled_before)
+            scaled_before = chunk
+        store_chunk(scaled_before)

@@ -230,17 +230,23 @@ def tile_mha_pa_t_kernel(tc, x, qkv, norm_w, out):
                     in_=to_store[:].rearrange("r i s e -> r i (s e)"),
                 )
 
-        load_half(0)
-        load_half(1)
         w_raw = const.tile([P, N_QKV, HEADS, PASSES, PACK, HEAD_DIM], BF16)
-        nc.scalar.dma_start(
-            out=w_raw[:],
-            in_=qkv.rearrange("n i (c p j) e -> p n i c j e", c=PASSES, p=P, j=PACK),
-        )
-        gain_bf16 = const.tile([P, 1], BF16)
-        nc.scalar.dma_start(out=gain_bf16[:], in_=norm_w.partition_broadcast(P))
+
+        def load_weights(n):
+            nc.sync.dma_start(
+                out=w_raw[:, n],
+                in_=qkv[n].rearrange("i (c p j) e -> p i c j e", c=PASSES, p=P, j=PACK),
+            )
+
+        load_half(0)
+        load_weights(0)
+        load_half(1)
+        for n in range(1, N_QKV):
+            load_weights(n)
         for half in range(2, LOADS_AHEAD):
             load_half(half)
+        gain_bf16 = const.tile([P, 1], BF16)
+        nc.sync.dma_start(out=gain_bf16[:], in_=norm_w.partition_broadcast(P))
 
         eps = const.tile([P, 1], F32)
         nc.vector.memset(eps[:], EPS)
@@ -249,7 +255,6 @@ def tile_mha_pa_t_kernel(tc, x, qkv, norm_w, out):
         identity = const.tile([P, P], F32)
         make_identity(nc, identity[:])
         gain = const.tile([P, 1], F32)
-        nc.scalar.copy(out=gain[:], in_=gain_bf16[:])
 
         w_grouped = const.tile([P, N_QKV, PASSES, HEADS, HEAD_DIM, PACK], BF16, align_bytes=64)
         w_codes = const.tile([P, N_QKV, PASSES, P], U32, align_bytes=64)
@@ -291,6 +296,8 @@ def tile_mha_pa_t_kernel(tc, x, qkv, norm_w, out):
 
             if step >= 1:
                 sum_squares_of_chunk(step - 1)
+                if step == CHUNKS:
+                    nc.scalar.copy(out=gain[:], in_=gain_bf16[:])
                 if step % CHUNKS == 0:
                     norm_factor_of_batch(step // CHUNKS - 1)
             if step >= SCALE_LAG:

@@ -32,6 +32,7 @@ STORE_LAG = SCALE_LAG + 1
 FIRST_HELPED = 3
 LAST_HELPED = 8
 HELP_PERIOD = 4
+HELP_END = HALVES - 4
 HELP_AHEAD = 4
 LINE_RUN = 4
 
@@ -79,7 +80,7 @@ def tile_mha_pa_t_kernel(tc, x, qkv, norm_w, out):
         def scalar_helps(half):
             if FIRST_HELPED <= half <= LAST_HELPED:
                 return True
-            return LAST_HELPED < half < HALVES and (half - LAST_HELPED) % HELP_PERIOD == 0
+            return LAST_HELPED < half < HELP_END and (half - LAST_HELPED) % HELP_PERIOD == 0
 
         def regroup_half_on_scalar(half):
             x_grouped = helped_pool.tile([P, CHUNK, PACK], BF16)

@@ -33,7 +33,7 @@ FIRST_HELPED = 3
 LAST_HELPED = 8
 HELP_PERIOD = 4
 HELP_END = HALVES - 4
-HELP_AHEAD = 4
+HELP_AHEAD = 6
 LINE_RUN = 4
 
 FLOPS = 2 * BATCH * SEQ * CHANNELS * N_QKV * HEADS * HEAD_DIM

@@ -26,6 +26,8 @@ RUN = CHUNK // P
 
 ALL_CHUNKS = BATCH * CHUNKS
 HALVES = ALL_CHUNKS * PASSES
+FIRST_PIECES = 2
+PIECE = CHUNK // FIRST_PIECES
 LOADS_AHEAD = 8
 SCALE_LAG = CHUNKS
 STORE_LAG = SCALE_LAG + 1
@@ -44,6 +46,7 @@ def tile_mha_pa_t_kernel(tc, x, qkv, norm_w, out):
     with ExitStack() as ctx:
         const = ctx.enter_context(tc.tile_pool(name="const", bufs=1))
         x_pool = ctx.enter_context(tc.tile_pool(name="x_pool", bufs=LOADS_AHEAD))
+        first_pool = ctx.enter_context(tc.tile_pool(name="first_pool", bufs=FIRST_PIECES))
         grouped_pool = ctx.enter_context(tc.tile_pool(name="grouped_pool", bufs=3))
         helped_pool = ctx.enter_context(tc.tile_pool(name="helped_pool", bufs=HELP_AHEAD + 2))
         fifth_pool = ctx.enter_context(tc.tile_pool(name="fifth_pool", bufs=2))
@@ -77,6 +80,17 @@ def tile_mha_pa_t_kernel(tc, x, qkv, norm_w, out):
             )
             x_tiles[half] = x_raw
 
+        def load_first_half():
+            pieces = []
+            for i in range(FIRST_PIECES):
+                x_piece = first_pool.tile([P, PACK, PIECE], BF16)
+                nc.sync.dma_start(
+                    out=x_piece[:],
+                    in_=x[0, 0:K_PASS, i * PIECE : (i + 1) * PIECE].rearrange("(p j) t -> p j t", j=PACK),
+                )
+                pieces.append(x_piece)
+            x_tiles[0] = pieces
+
         def scalar_helps(half):
             if FIRST_HELPED <= half <= LAST_HELPED:
                 return True
@@ -101,15 +115,20 @@ def tile_mha_pa_t_kernel(tc, x, qkv, norm_w, out):
                 fifth_tiles[half] = fifth
             else:
                 a_grouped = grouped_pool.tile([P, CHUNK * PACK], BF16, align_bytes=64)
-                x_by_position = x_tiles[half][:].rearrange("p j t -> p t j")
-                nc.vector.scalar_tensor_tensor(
-                    out=a_grouped[:].rearrange("p (t j) -> p t j", j=PACK),
-                    in0=x_by_position,
-                    scalar=NEG_SLOPE,
-                    in1=x_by_position,
-                    op0=ALU.mult,
-                    op1=ALU.max,
-                )
+                pieces = x_tiles[half] if half == 0 else [x_tiles[half]]
+                width = CHUNK * PACK // len(pieces)
+                for i, x_piece in enumerate(pieces):
+                    x_by_position = x_piece[:].rearrange("p j t -> p t j")
+                    nc.vector.scalar_tensor_tensor(
+                        out=a_grouped[:, i * width : (i + 1) * width].rearrange(
+                            "p (t j) -> p t j", j=PACK
+                        ),
+                        in0=x_by_position,
+                        scalar=NEG_SLOPE,
+                        in1=x_by_position,
+                        op0=ALU.mult,
+                        op1=ALU.max,
+                    )
                 grouped_tiles[half] = a_grouped
 
         def end_leaky_relu(half):
@@ -239,7 +258,7 @@ def tile_mha_pa_t_kernel(tc, x, qkv, norm_w, out):
                 in_=qkv[n].rearrange("i (c p j) e -> p i c j e", c=PASSES, p=P, j=PACK),
             )
 
-        load_half(0)
+        load_first_half()
         load_weights(0)
         load_half(1)
         for n in range(1, N_QKV):

@@ -28,7 +28,7 @@ ALL_CHUNKS = BATCH * CHUNKS
 HALVES = ALL_CHUNKS * PASSES
 FIRST_PIECES = 2
 PIECE = CHUNK // FIRST_PIECES
-LOADS_AHEAD = 8
+LOADS_AHEAD = 12
 SCALE_LAG = CHUNKS
 STORE_LAG = SCALE_LAG + 1
 FIRST_HELPED = 3
@@ -36,7 +36,7 @@ LAST_HELPED = 8
 HELP_PERIOD = 4
 HELP_END = HALVES - 4
 HELP_AHEAD = 6
-LINE_RUN = 4
+LINE_RUN = 8
 
 FLOPS = 2 * BATCH * SEQ * CHANNELS * N_QKV * HEADS * HEAD_DIM
 
@@ -80,16 +80,13 @@ def tile_mha_pa_t_kernel(tc, x, qkv, norm_w, out):
             )
             x_tiles[half] = x_raw
 
-        def load_first_half():
-            pieces = []
-            for i in range(FIRST_PIECES):
-                x_piece = first_pool.tile([P, PACK, PIECE], BF16)
-                nc.sync.dma_start(
-                    out=x_piece[:],
-                    in_=x[0, 0:K_PASS, i * PIECE : (i + 1) * PIECE].rearrange("(p j) t -> p j t", j=PACK),
-                )
-                pieces.append(x_piece)
-            x_tiles[0] = pieces
+        def load_first_half(i):
+            x_piece = first_pool.tile([P, PACK, PIECE], BF16)
+            nc.sync.dma_start(
+                out=x_piece[:],
+                in_=x[0, 0:K_PASS, i * PIECE : (i + 1) * PIECE].rearrange("(p j) t -> p j t", j=PACK),
+            )
+            x_tiles.setdefault(0, []).append(x_piece)
 
         def scalar_helps(half):
             if FIRST_HELPED <= half <= LAST_HELPED:
@@ -258,8 +255,9 @@ def tile_mha_pa_t_kernel(tc, x, qkv, norm_w, out):
                 in_=qkv[n].rearrange("i (c p j) e -> p i c j e", c=PASSES, p=P, j=PACK),
             )
 
-        load_first_half()
+        load_first_half(0)
         load_weights(0)
+        load_first_half(1)
         load_half(1)
         for n in range(1, N_QKV):
             load_weights(n)

@@ -28,16 +28,20 @@ ALL_CHUNKS = BATCH * CHUNKS
 HALVES = ALL_CHUNKS * PASSES
 FIRST_PIECES = 2
 PIECE = CHUNK // FIRST_PIECES
-LOADS_AHEAD = 12
+LOADS_AHEAD = 8
 SCALE_LAG = CHUNKS
 STORE_LAG = SCALE_LAG + 1
 FIRST_HELPED = 3
 LAST_HELPED = 8
-HELP_PERIOD = 4
+HELP_PERIOD = 99
 HELP_END = HALVES - 4
 HELP_AHEAD = 6
 LINE_RUN = 8
 
+LATE = (24, 25, 26, 27)
+LATE_FROM, LATE_EVERY = 10, 3
+DIRECT = (13, 12)
+LATE_LOADS = 2
 FLOPS = 2 * BATCH * SEQ * CHANNELS * N_QKV * HEADS * HEAD_DIM
 
 
@@ -47,6 +51,9 @@ def tile_mha_pa_t_kernel(tc, x, qkv, norm_w, out):
         const = ctx.enter_context(tc.tile_pool(name="const", bufs=1))
         x_pool = ctx.enter_context(tc.tile_pool(name="x_pool", bufs=LOADS_AHEAD))
         first_pool = ctx.enter_context(tc.tile_pool(name="first_pool", bufs=FIRST_PIECES))
+        late_pool = ctx.enter_context(tc.tile_pool(name="late_pool", bufs=LATE_LOADS))
+        late_helped_pool = ctx.enter_context(tc.tile_pool(name="late_helped_pool", bufs=len(LATE)))
+        rows_pool = ctx.enter_context(tc.tile_pool(name="rows_pool", bufs=N_QKV))
         grouped_pool = ctx.enter_context(tc.tile_pool(name="grouped_pool", bufs=3))
         helped_pool = ctx.enter_context(tc.tile_pool(name="helped_pool", bufs=HELP_AHEAD + 2))
         fifth_pool = ctx.enter_context(tc.tile_pool(name="fifth_pool", bufs=2))
@@ -54,7 +61,7 @@ def tile_mha_pa_t_kernel(tc, x, qkv, norm_w, out):
         stats_pool = ctx.enter_context(tc.tile_pool(name="stats_pool", bufs=2))
         squares_pool = ctx.enter_context(tc.tile_pool(name="squares_pool", bufs=3))
         scaled_pool = ctx.enter_context(tc.tile_pool(name="scaled_pool", bufs=2 * N_QKV + 2))
-        store_pool = ctx.enter_context(tc.tile_pool(name="store_pool", bufs=2 * N_QKV))
+        store_pool = ctx.enter_context(tc.tile_pool(name="store_pool", bufs=3 * N_QKV))
         psum_products = ctx.enter_context(tc.psum_pool(name="psum_products", bufs=5))
         psum_turned = ctx.enter_context(tc.psum_pool(name="psum_turned", bufs=3))
         ctx.enter_context(tc.manual_schedule())
@@ -66,12 +73,16 @@ def tile_mha_pa_t_kernel(tc, x, qkv, norm_w, out):
         code_tiles = {}
         sum_tiles = {}
         factor_tiles = {}
+        turned_tiles = {}
         scaled_tiles = {}
 
         def load_half(half):
             chunk, c = divmod(half, PASSES)
             b, q = divmod(chunk, CHUNKS)
-            x_raw = x_pool.tile([P, PACK, CHUNK], BF16)
+            if half in LATE:
+                x_raw = late_pool.tile([P, PACK, CHUNK], BF16)
+            else:
+                x_raw = x_pool.tile([P, PACK, CHUNK], BF16)
             nc.sync.dma_start(
                 out=x_raw[:],
                 in_=x[
@@ -80,21 +91,29 @@ def tile_mha_pa_t_kernel(tc, x, qkv, norm_w, out):
             )
             x_tiles[half] = x_raw
 
-        def load_first_half(i):
-            x_piece = first_pool.tile([P, PACK, PIECE], BF16)
-            nc.sync.dma_start(
-                out=x_piece[:],
-                in_=x[0, 0:K_PASS, i * PIECE : (i + 1) * PIECE].rearrange("(p j) t -> p j t", j=PACK),
-            )
-            x_tiles.setdefault(0, []).append(x_piece)
+        def load_first_half():
+            pieces = []
+            for i in range(FIRST_PIECES):
+                x_piece = first_pool.tile([P, PACK, PIECE], BF16)
+                nc.sync.dma_start(
+                    out=x_piece[:],
+                    in_=x[0, 0:K_PASS, i * PIECE : (i + 1) * PIECE].rearrange("(p j) t -> p j t", j=PACK),
+                )
+                pieces.append(x_piece)
+            x_tiles[0] = pieces
 
         def scalar_helps(half):
+            if half in LATE:
+                return True
             if FIRST_HELPED <= half <= LAST_HELPED:
                 return True
             return LAST_HELPED < half < HELP_END and (half - LAST_HELPED) % HELP_PERIOD == 0
 
         def regroup_half_on_scalar(half):
-            x_grouped = helped_pool.tile([P, CHUNK, PACK], BF16)
+            if half in LATE:
+                x_grouped = late_helped_pool.tile([P, CHUNK, PACK], BF16)
+            else:
+                x_grouped = helped_pool.tile([P, CHUNK, PACK], BF16)
             nc.scalar.copy(
                 out=x_grouped[:].rearrange("p (g i) j -> p g j i", i=LINE_RUN),
                 in_=x_tiles[half][:].rearrange("p j (g i) -> p g j i", i=LINE_RUN),
@@ -131,11 +150,18 @@ def tile_mha_pa_t_kernel(tc, x, qkv, norm_w, out):
         def end_leaky_relu(half):
             if scalar_helps(half):
                 a_grouped = grouped_pool.tile([P, CHUNK * PACK], BF16, align_bytes=64)
-                nc.vector.tensor_max(
-                    out=a_grouped[:],
-                    in0=regrouped_tiles[half][:].rearrange("p t j -> p (t j)"),
-                    in1=fifth_tiles[half][:],
-                )
+                if half // PASSES in DIRECT:
+                    nc.vector.tensor_max(
+                        out=a_grouped[:].rearrange("p (s r j) -> p s r j", s=RUN, j=PACK),
+                        in0=regrouped_tiles[half][:].rearrange("p (r s) j -> p s r j", s=RUN),
+                        in1=fifth_tiles[half][:].rearrange("p (r s j) -> p s r j", s=RUN, j=PACK),
+                    )
+                else:
+                    nc.vector.tensor_max(
+                        out=a_grouped[:],
+                        in0=regrouped_tiles[half][:].rearrange("p t j -> p (t j)"),
+                        in1=fifth_tiles[half][:],
+                    )
                 grouped_tiles[half] = a_grouped
 
         def quantise_half(half):
@@ -168,23 +194,23 @@ def tile_mha_pa_t_kernel(tc, x, qkv, norm_w, out):
                 )
             return h
 
+        def sum_squares(chunk, n, h):
+            b, q = divmod(chunk, CHUNKS)
+            squares = squares_pool.tile([P, CHUNK], BF16)
+            nc.scalar.activation(
+                out=squares[:],
+                in_=h[:],
+                func=ACT.Square,
+                accum_out=sum_tiles[b][:, n, q : q + 1],
+            )
+
         def sum_squares_of_chunk(chunk):
             b, q = divmod(chunk, CHUNKS)
             if q == 0:
-                sum_squares = stats_pool.tile([P, N_QKV, CHUNKS], F32)
-                sum_tiles[b] = sum_squares
-            products = []
+                sum_tile = stats_pool.tile([P, N_QKV, CHUNKS], F32)
+                sum_tiles[b] = sum_tile
             for n in range(N_QKV):
-                h = project(chunk, n)
-                squares = squares_pool.tile([P, CHUNK], BF16)
-                nc.scalar.activation(
-                    out=squares[:],
-                    in_=h[:],
-                    func=ACT.Square,
-                    accum_out=sum_tiles[b][:, n, q : q + 1],
-                )
-                products.append(h)
-            return products
+                sum_squares(chunk, n, project(chunk, n))
 
         def norm_factor_of_batch(b):
             total = stats_pool.tile([P, N_QKV], F32)
@@ -210,42 +236,86 @@ def tile_mha_pa_t_kernel(tc, x, qkv, norm_w, out):
             )
             factor_tiles[b] = factor
 
-        def scale_chunk(chunk, vector_is_free, products=None):
-            b = chunk // CHUNKS
-            for n in range(N_QKV):
-                h = products[n] if products else project(chunk, n)
-                h_by_block = h[:].rearrange("m (r s) -> m s r", s=RUN)
-                h_scaled = scaled_pool.tile([P, RUN, P], F32)
-                if vector_is_free:
-                    nc.vector.tensor_scalar_mul(
-                        out=h_scaled[:], in0=h_by_block, scalar1=factor_tiles[b][:, n : n + 1]
-                    )
-                else:
-                    nc.scalar.activation(
-                        out=h_scaled[:],
-                        in_=h_by_block,
-                        func=ACT.Copy,
-                        scale=factor_tiles[b][:, n : n + 1],
-                    )
-                scaled_tiles[(chunk, n)] = h_scaled
+        def scale(chunk, n, h, scale_out):
+            h_scaled = scaled_pool.tile([P, RUN, P], F32)
+            scale_out(h_scaled[:], h[:].rearrange("m (r s) -> m s r", s=RUN))
+            scaled_tiles[(chunk, n)] = h_scaled
 
-        def store_chunk(chunk):
+        def scale_on_scalar(b, n):
+            factor = factor_tiles[b][:, n : n + 1]
+            return lambda to, h: nc.scalar.activation(out=to, in_=h, func=ACT.Copy, scale=factor)
+
+        def scale_on_vector(b, n):
+            factor = factor_tiles[b][:, n : n + 1]
+            return lambda to, h: nc.vector.tensor_scalar_mul(out=to, in0=h, scalar1=factor)
+
+        def turn(chunk, n):
+            h_scaled = scaled_tiles[(chunk, n)]
+            turned = psum_turned.tile([P, RUN, P], F32)
+            for s in range(RUN):
+                nc.tensor.transpose(turned[:, s, :], h_scaled[:, s, :], identity[:])
+            turned_tiles[(chunk, n)] = turned
+
+        def store(chunk, n, copy=nc.scalar.copy):
             b, q = divmod(chunk, CHUNKS)
+            to_store = store_pool.tile([P, HEADS, RUN, HEAD_DIM], F32)
+            copy(
+                out=to_store[:],
+                in_=turned_tiles[(chunk, n)][:].rearrange("r s (i e) -> r i s e", i=HEADS),
+            )
+            nc.sync.dma_start(
+                out=out[n, b, :, q * CHUNK : (q + 1) * CHUNK, :].rearrange(
+                    "i (r s) e -> r i (s e)", s=RUN
+                ),
+                in_=to_store[:].rearrange("r i s e -> r i (s e)"),
+            )
+
+        def turn_and_store(chunk, copy=nc.scalar.copy):
             for n in range(N_QKV):
-                h_scaled = scaled_tiles[(chunk, n)]
-                turned = psum_turned.tile([P, RUN, P], F32)
-                for s in range(RUN):
-                    nc.tensor.transpose(turned[:, s, :], h_scaled[:, s, :], identity[:])
-                to_store = store_pool.tile([P, HEADS, RUN, HEAD_DIM], F32)
-                nc.scalar.copy(
-                    out=to_store[:], in_=turned[:].rearrange("r s (i e) -> r i s e", i=HEADS)
-                )
-                nc.sync.dma_start(
-                    out=out[n, b, :, q * CHUNK : (q + 1) * CHUNK, :].rearrange(
-                        "i (r s) e -> r i (s e)", s=RUN
-                    ),
-                    in_=to_store[:].rearrange("r i s e -> r i (s e)"),
-                )
+                turn(chunk, n)
+                store(chunk, n, copy)
+
+        def spread(column, scale=1.0):
+            turned = psum_turned.tile([P, P], F32)
+            nc.tensor.transpose(turned[:], column.to_broadcast([P, P]), identity[:])
+            row = rows_pool.tile([P, P], F32)
+            nc.scalar.activation(out=row[:], in_=turned[:], func=ACT.Copy, scale=scale)
+            return row
+
+        def multiply_direct(chunk, n):
+            b, q = divmod(chunk, CHUNKS)
+            a_codes, a_scales = code_tiles[b]
+            h = psum_products.tile([P, RUN, P], F32)
+            for s in range(RUN):
+                for c in range(PASSES):
+                    nc.tensor.matmul_mx(
+                        out=h[:, s, :],
+                        lhsT=a_codes[:, q, c, s * P : (s + 1) * P].bitcast(FP8X4),
+                        lhsT_scale=a_scales[:, q, c, s * P : (s + 1) * P],
+                        rhs=w_codes[:, n, c, :].bitcast(FP8X4),
+                        rhs_scale=w_scales[:, n, c, :],
+                        start=(c == 0),
+                        stop=(c == PASSES - 1),
+                    )
+            return h
+
+        def store_direct(chunk, n, h, row):
+            b, q = divmod(chunk, CHUNKS)
+            to_store = store_pool.tile([P, HEADS, RUN, HEAD_DIM], F32)
+            nc.vector.tensor_mul(
+                out=to_store[:].rearrange("r i s e -> r s i e"),
+                in0=h[:].rearrange("r s (i e) -> r s i e", i=HEADS),
+                in1=row[:]
+                .rearrange("r (i e) -> r i e", i=HEADS)
+                .unsqueeze(1)
+                .to_broadcast([P, RUN, HEADS, HEAD_DIM]),
+            )
+            nc.sync.dma_start(
+                out=out[n, b, :, q * CHUNK : (q + 1) * CHUNK, :].rearrange(
+                    "i (r s) e -> r i (s e)", s=RUN
+                ),
+                in_=to_store[:].rearrange("r i s e -> r i (s e)"),
+            )
 
         w_raw = const.tile([P, N_QKV, HEADS, PASSES, PACK, HEAD_DIM], BF16)
 
@@ -255,9 +325,8 @@ def tile_mha_pa_t_kernel(tc, x, qkv, norm_w, out):
                 in_=qkv[n].rearrange("i (c p j) e -> p i c j e", c=PASSES, p=P, j=PACK),
             )
 
-        load_first_half(0)
+        load_first_half()
         load_weights(0)
-        load_first_half(1)
         load_half(1)
         for n in range(1, N_QKV):
             load_weights(n)
@@ -298,18 +367,25 @@ def tile_mha_pa_t_kernel(tc, x, qkv, norm_w, out):
 
         for step in range(ALL_CHUNKS):
             for half in range(PASSES * step, PASSES * (step + 1)):
-                if scalar_helps(half + HELP_AHEAD):
+                if half + HELP_AHEAD not in LATE and scalar_helps(half + HELP_AHEAD):
                     regroup_half_on_scalar(half + HELP_AHEAD)
+                k, rest = divmod(half - LATE_FROM, LATE_EVERY)
+                if rest == 0 and 0 <= k < len(LATE):
+                    regroup_half_on_scalar(LATE[k])
+                    if k + LATE_LOADS < len(LATE):
+                        load_half(LATE[k + LATE_LOADS])
+                if half == 1:
+                    for k in range(LATE_LOADS):
+                        load_half(LATE[k])
                 begin_leaky_relu(half)
-                if half + LOADS_AHEAD < HALVES:
+                if half + LOADS_AHEAD < HALVES and half + LOADS_AHEAD not in LATE:
                     load_half(half + LOADS_AHEAD)
                 if half >= 1:
                     quantise_half(half - 1)
                 end_leaky_relu(half)
                 if half == PASSES:
                     quantise_weights()
-            vector_is_free = step == ALL_CHUNKS - 1
-            if vector_is_free:
+            if step == ALL_CHUNKS - 1:
                 quantise_half(HALVES - 1)
 
             if step >= 1:
@@ -318,19 +394,129 @@ def tile_mha_pa_t_kernel(tc, x, qkv, norm_w, out):
                     nc.scalar.copy(out=gain[:], in_=gain_bf16[:])
                 if step % CHUNKS == 0:
                     norm_factor_of_batch(step // CHUNKS - 1)
-            if step >= SCALE_LAG:
-                scale_chunk(step - SCALE_LAG, vector_is_free)
-            if step >= STORE_LAG:
-                store_chunk(step - STORE_LAG)
+            if SCALE_LAG <= step < ALL_CHUNKS - 1:
+                chunk = step - SCALE_LAG
+                for n in range(N_QKV):
+                    scale(chunk, n, project(chunk, n), scale_on_scalar(chunk // CHUNKS, n))
+            if STORE_LAG <= step < ALL_CHUNKS - 1:
+                turn_and_store(step - STORE_LAG)
 
-        last = ALL_CHUNKS - 1
-        last_products = sum_squares_of_chunk(last)
-        norm_factor_of_batch(BATCH - 1)
-        store_chunk(last - SCALE_LAG)
-        scale_chunk(last, True, last_products)
-        scaled_before = last
-        for chunk in range(last - CHUNKS + 1, last):
-            scale_chunk(chunk, True)
-            store_chunk(scaled_before)
-            scaled_before = chunk
-        store_chunk(scaled_before)
+        b, last = BATCH - 1, ALL_CHUNKS - 1
+        first = last - CHUNKS + 1
+        mean_before = stats_pool.tile([P, N_QKV], F32)
+        addends = stats_pool.tile([P, N_QKV, CHUNKS - 1], F32)
+        mean_and_eps = stats_pool.tile([P, N_QKV], F32)
+        inverse_rms = [stats_pool.tile([P, 1], F32, name="inverse_rms_%d" % n) for n in range(N_QKV)]
+        products = {}
+        rows = {}
+
+        def mean_without_last_chunk():
+            for n in range(N_QKV):
+                nc.scalar.activation(
+                    out=addends[:, n, :],
+                    in_=sum_tiles[b][:, n, 0 : CHUNKS - 1],
+                    func=ACT.Copy,
+                    scale=1.0 / SEQ,
+                    accum_out=mean_before[:, n : n + 1],
+                )
+            nc.scalar.activation(
+                out=mean_and_eps[:], in_=mean_before[:], func=ACT.Identity, bias=eps[:, 0:1]
+            )
+
+        def scale_by_parts(n):
+            return lambda to, h: nc.vector.tensor_scalar(
+                out=to,
+                in0=h,
+                scalar1=inverse_rms[n][:, 0:1],
+                scalar2=gain[:, 0:1],
+                op0=ALU.mult,
+                op1=ALU.mult,
+            )
+
+        def form(chunk, *ns):
+            for n in ns:
+                make = multiply_direct if chunk in DIRECT else project
+                products[(chunk, n)] = make(chunk, n)
+
+        def scale_late(chunk, *ns):
+            for n in ns:
+                how = scale_by_parts(n) if chunk >= first else scale_on_vector(b - 1, n)
+                scale(chunk, n, products[(chunk, n)], how)
+
+        def turn_all(chunk, *ns):
+            for n in ns:
+                turn(chunk, n)
+
+        def store_all(chunk, *ns, copy=nc.scalar.copy):
+            for n in ns:
+                store(chunk, n, copy)
+
+        def square(n):
+            sum_squares(last, n, products[(last, n)])
+
+        def root(n):
+            nc.scalar.activation(
+                out=inverse_rms[n][:],
+                in_=sum_tiles[b][:, n, CHUNKS - 1 : CHUNKS],
+                func=ACT.Abs_reciprocal_sqrt,
+                scale=1.0 / SEQ,
+                bias=mean_and_eps[:, n : n + 1],
+            )
+
+        def spread_row(n):
+            rows[n] = spread(inverse_rms[n][:], gain[:, 0:1])
+
+        def direct(n):
+            for chunk in DIRECT:
+                store_direct(chunk, n, products[(chunk, n)], rows[n])
+
+        everything = range(N_QKV)
+        form(first - 1, 0, 1)
+        turn_all(first - 2, *everything)
+        scale_late(first - 1, 0, 1)
+        store_all(first - 2, *everything, copy=nc.vector.tensor_copy)
+        mean_without_last_chunk()
+        form(last, *everything)
+        form(first - 1, 2)
+        scale_late(first - 1, 2)
+        square(0)
+        root(0)
+        square(1)
+        root(1)
+        turn_all(first - 1, 0)
+        form(first, 0)
+        store_all(first - 1, 0)
+        scale_late(last, 0)
+        square(2)
+        spread_row(0)
+        root(2)
+        turn_all(first - 1, 1, 2)
+        scale_late(last, 1, 2)
+        store_all(first - 1, 1, 2)
+        turn_all(last, 0)
+        spread_row(1)
+        store_all(last, 0)
+        form(last - 1, 0)
+        form(first + 1, 0)
+        turn_all(last, 1)
+        spread_row(2)
+        store_all(last, 1)
+        direct(0)
+        scale_late(last - 1, 0)
+        form(first + 1, 1)
+        form(first, 1)
+        turn_all(last, 2)
+        turn_all(last - 1, 0)
+        store_all(last, 2)
+        store_all(last - 1, 0)
+        direct(1)
+        form(last - 1, 1)
+        form(first + 1, 2)
+        form(first, 2)
+        form(last - 1, 2)
+        scale_late(last - 1, 1)
+        turn_all(last - 1, 1)
+        direct(2)
+        scale_late(last - 1, 2)
+        turn_all(last - 1, 2)
+        store_all(last - 1, 1, 2)

@@ -152,9 +152,9 @@ def tile_mha_pa_t_kernel(tc, x, qkv, norm_w, out):
                 a_grouped = grouped_pool.tile([P, CHUNK * PACK], BF16, align_bytes=64)
                 if half // PASSES in DIRECT:
                     nc.vector.tensor_max(
-                        out=a_grouped[:].rearrange("p (s r j) -> p s r j", s=RUN, j=PACK),
-                        in0=regrouped_tiles[half][:].rearrange("p (r s) j -> p s r j", s=RUN),
-                        in1=fifth_tiles[half][:].rearrange("p (r s j) -> p s r j", s=RUN, j=PACK),
+                        out=a_grouped[:].rearrange("p (s r j) -> p r s j", s=RUN, j=PACK),
+                        in0=regrouped_tiles[half][:].rearrange("p (r s) j -> p r s j", s=RUN),
+                        in1=fifth_tiles[half][:].rearrange("p (r s j) -> p r s j", s=RUN, j=PACK),
                     )
                 else:
                     nc.vector.tensor_max(

from contextlib import ExitStack

import concourse.mybir as mybir
from concourse.masks import make_identity

BF16 = mybir.dt.bfloat16
F32 = mybir.dt.float32
U32 = mybir.dt.uint32
U8 = mybir.dt.uint8
FP8X4 = mybir.dt.float8_e4m3fn_x4
ACT = mybir.ActivationFunctionType
ALU = mybir.AluOpType

BATCH, CHANNELS, SEQ = 4, 1024, 2048
N_QKV, HEADS, HEAD_DIM = 3, 2, 64
NEG_SLOPE = 0.2
EPS = 1e-6

P = 128
PACK = 4
K_PASS = P * PACK
PASSES = CHANNELS // K_PASS
CHUNK = 512
CHUNKS = SEQ // CHUNK
RUN = CHUNK // P

ALL_CHUNKS = BATCH * CHUNKS
HALVES = ALL_CHUNKS * PASSES
FIRST_PIECES = 2
PIECE = CHUNK // FIRST_PIECES
LOADS_AHEAD = 8
SCALE_LAG = CHUNKS
STORE_LAG = SCALE_LAG + 1
FIRST_HELPED = 3
LAST_HELPED = 8
HELP_PERIOD = 99
HELP_END = HALVES - 4
HELP_AHEAD = 6
LINE_RUN = 8

LATE = (24, 25, 26, 27)
LATE_FROM, LATE_EVERY = 10, 3
DIRECT = (13, 12)
LATE_LOADS = 2
FLOPS = 2 * BATCH * SEQ * CHANNELS * N_QKV * HEADS * HEAD_DIM


def tile_mha_pa_t_kernel(tc, x, qkv, norm_w, out):
    nc = tc.nc
    with ExitStack() as ctx:
        const = ctx.enter_context(tc.tile_pool(name="const", bufs=1))
        x_pool = ctx.enter_context(tc.tile_pool(name="x_pool", bufs=LOADS_AHEAD))
        first_pool = ctx.enter_context(tc.tile_pool(name="first_pool", bufs=FIRST_PIECES))
        late_pool = ctx.enter_context(tc.tile_pool(name="late_pool", bufs=LATE_LOADS))
        late_helped_pool = ctx.enter_context(tc.tile_pool(name="late_helped_pool", bufs=len(LATE)))
        rows_pool = ctx.enter_context(tc.tile_pool(name="rows_pool", bufs=N_QKV))
        grouped_pool = ctx.enter_context(tc.tile_pool(name="grouped_pool", bufs=3))
        helped_pool = ctx.enter_context(tc.tile_pool(name="helped_pool", bufs=HELP_AHEAD + 2))
        fifth_pool = ctx.enter_context(tc.tile_pool(name="fifth_pool", bufs=2))
        codes_pool = ctx.enter_context(tc.tile_pool(name="codes_pool", bufs=3))
        stats_pool = ctx.enter_context(tc.tile_pool(name="stats_pool", bufs=2))
        squares_pool = ctx.enter_context(tc.tile_pool(name="squares_pool", bufs=3))
        scaled_pool = ctx.enter_context(tc.tile_pool(name="scaled_pool", bufs=2 * N_QKV + 2))
        store_pool = ctx.enter_context(tc.tile_pool(name="store_pool", bufs=3 * N_QKV))
        psum_products = ctx.enter_context(tc.psum_pool(name="psum_products", bufs=5))
        psum_turned = ctx.enter_context(tc.psum_pool(name="psum_turned", bufs=3))
        ctx.enter_context(tc.manual_schedule())

        x_tiles = {}
        regrouped_tiles = {}
        fifth_tiles = {}
        grouped_tiles = {}
        code_tiles = {}
        sum_tiles = {}
        factor_tiles = {}
        turned_tiles = {}
        scaled_tiles = {}

        def load_half(half):
            chunk, c = divmod(half, PASSES)
            b, q = divmod(chunk, CHUNKS)
            if half in LATE:
                x_raw = late_pool.tile([P, PACK, CHUNK], BF16)
            else:
                x_raw = x_pool.tile([P, PACK, CHUNK], BF16)
            nc.sync.dma_start(
                out=x_raw[:],
                in_=x[
                    b, c * K_PASS : (c + 1) * K_PASS, q * CHUNK : (q + 1) * CHUNK
                ].rearrange("(p j) t -> p j t", j=PACK),
            )
            x_tiles[half] = x_raw

        def load_first_half():
            pieces = []
            for i in range(FIRST_PIECES):
                x_piece = first_pool.tile([P, PACK, PIECE], BF16)
                nc.sync.dma_start(
                    out=x_piece[:],
                    in_=x[0, 0:K_PASS, i * PIECE : (i + 1) * PIECE].rearrange("(p j) t -> p j t", j=PACK),
                )
                pieces.append(x_piece)
            x_tiles[0] = pieces

        def scalar_helps(half):
            if half in LATE:
                return True
            if FIRST_HELPED <= half <= LAST_HELPED:
                return True
            return LAST_HELPED < half < HELP_END and (half - LAST_HELPED) % HELP_PERIOD == 0

        def regroup_half_on_scalar(half):
            if half in LATE:
                x_grouped = late_helped_pool.tile([P, CHUNK, PACK], BF16)
            else:
                x_grouped = helped_pool.tile([P, CHUNK, PACK], BF16)
            nc.scalar.copy(
                out=x_grouped[:].rearrange("p (g i) j -> p g j i", i=LINE_RUN),
                in_=x_tiles[half][:].rearrange("p j (g i) -> p g j i", i=LINE_RUN),
            )
            regrouped_tiles[half] = x_grouped

        def begin_leaky_relu(half):
            if scalar_helps(half):
                fifth = fifth_pool.tile([P, CHUNK * PACK], BF16)
                nc.vector.tensor_scalar_mul(
                    out=fifth[:],
                    in0=regrouped_tiles[half][:].rearrange("p t j -> p (t j)"),
                    scalar1=NEG_SLOPE,
                )
                fifth_tiles[half] = fifth
            else:
                a_grouped = grouped_pool.tile([P, CHUNK * PACK], BF16, align_bytes=64)
                pieces = x_tiles[half] if half == 0 else [x_tiles[half]]
                width = CHUNK * PACK // len(pieces)
                for i, x_piece in enumerate(pieces):
                    x_by_position = x_piece[:].rearrange("p j t -> p t j")
                    nc.vector.scalar_tensor_tensor(
                        out=a_grouped[:, i * width : (i + 1) * width].rearrange(
                            "p (t j) -> p t j", j=PACK
                        ),
                        in0=x_by_position,
                        scalar=NEG_SLOPE,
                        in1=x_by_position,
                        op0=ALU.mult,
                        op1=ALU.max,
                    )
                grouped_tiles[half] = a_grouped

        def end_leaky_relu(half):
            if scalar_helps(half):
                a_grouped = grouped_pool.tile([P, CHUNK * PACK], BF16, align_bytes=64)
                if half // PASSES in DIRECT:
                    nc.vector.tensor_max(
                        out=a_grouped[:].rearrange("p (s r j) -> p r s j", s=RUN, j=PACK),
                        in0=regrouped_tiles[half][:].rearrange("p (r s) j -> p r s j", s=RUN),
                        in1=fifth_tiles[half][:].rearrange("p (r s j) -> p r s j", s=RUN, j=PACK),
                    )
                else:
                    nc.vector.tensor_max(
                        out=a_grouped[:],
                        in0=regrouped_tiles[half][:].rearrange("p t j -> p (t j)"),
                        in1=fifth_tiles[half][:],
                    )
                grouped_tiles[half] = a_grouped

        def quantise_half(half):
            chunk, c = divmod(half, PASSES)
            b, q = divmod(chunk, CHUNKS)
            if b not in code_tiles:
                a_codes = codes_pool.tile([P, CHUNKS, PASSES, CHUNK], U32, align_bytes=64)
                a_scales = codes_pool.tile([P, CHUNKS, PASSES, CHUNK], U8, align_bytes=64)
                code_tiles[b] = (a_codes, a_scales)
            a_codes, a_scales = code_tiles[b]
            nc.vector.quantize_mx(
                out=a_codes[:, q, c, :].bitcast(FP8X4),
                scales=a_scales[:, q, c, :],
                in_=grouped_tiles[half][:],
            )

        def project(chunk, n):
            b, q = divmod(chunk, CHUNKS)
            a_codes, a_scales = code_tiles[b]
            h = psum_products.tile([P, CHUNK], F32)
            for c in range(PASSES):
                nc.tensor.matmul_mx(
                    out=h[:],
                    lhsT=w_codes[:, n, c, :].bitcast(FP8X4),
                    lhsT_scale=w_scales[:, n, c, :],
                    rhs=a_codes[:, q, c, :].bitcast(FP8X4),
                    rhs_scale=a_scales[:, q, c, :],
                    start=(c == 0),
                    stop=(c == PASSES - 1),
                )
            return h

        def sum_squares(chunk, n, h):
            b, q = divmod(chunk, CHUNKS)
            squares = squares_pool.tile([P, CHUNK], BF16)
            nc.scalar.activation(
                out=squares[:],
                in_=h[:],
                func=ACT.Square,
                accum_out=sum_tiles[b][:, n, q : q + 1],
            )

        def sum_squares_of_chunk(chunk):
            b, q = divmod(chunk, CHUNKS)
            if q == 0:
                sum_tile = stats_pool.tile([P, N_QKV, CHUNKS], F32)
                sum_tiles[b] = sum_tile
            for n in range(N_QKV):
                sum_squares(chunk, n, project(chunk, n))

        def norm_factor_of_batch(b):
            total = stats_pool.tile([P, N_QKV], F32)
            copied = stats_pool.tile([P, N_QKV, CHUNKS], F32)
            for n in range(N_QKV):
                nc.scalar.activation(
                    out=copied[:, n, :],
                    in_=sum_tiles[b][:, n, :],
                    func=ACT.Copy,
                    accum_out=total[:, n : n + 1],
                )
            inverse_rms = stats_pool.tile([P, N_QKV], F32)
            nc.scalar.activation(
                out=inverse_rms[:],
                in_=total[:],
                func=ACT.Abs_reciprocal_sqrt,
                scale=1.0 / SEQ,
                bias=eps[:, 0:1],
            )
            factor = stats_pool.tile([P, N_QKV], F32)
            nc.scalar.activation(
                out=factor[:], in_=inverse_rms[:], func=ACT.Copy, scale=gain[:, 0:1]
            )
            factor_tiles[b] = factor

        def scale(chunk, n, h, scale_out):
            h_scaled = scaled_pool.tile([P, RUN, P], F32)
            scale_out(h_scaled[:], h[:].rearrange("m (r s) -> m s r", s=RUN))
            scaled_tiles[(chunk, n)] = h_scaled

        def scale_on_scalar(b, n):
            factor = factor_tiles[b][:, n : n + 1]
            return lambda to, h: nc.scalar.activation(out=to, in_=h, func=ACT.Copy, scale=factor)

        def scale_on_vector(b, n):
            factor = factor_tiles[b][:, n : n + 1]
            return lambda to, h: nc.vector.tensor_scalar_mul(out=to, in0=h, scalar1=factor)

        def turn(chunk, n):
            h_scaled = scaled_tiles[(chunk, n)]
            turned = psum_turned.tile([P, RUN, P], F32)
            for s in range(RUN):
                nc.tensor.transpose(turned[:, s, :], h_scaled[:, s, :], identity[:])
            turned_tiles[(chunk, n)] = turned

        def store(chunk, n, copy=nc.scalar.copy):
            b, q = divmod(chunk, CHUNKS)
            to_store = store_pool.tile([P, HEADS, RUN, HEAD_DIM], F32)
            copy(
                out=to_store[:],
                in_=turned_tiles[(chunk, n)][:].rearrange("r s (i e) -> r i s e", i=HEADS),
            )
            nc.sync.dma_start(
                out=out[n, b, :, q * CHUNK : (q + 1) * CHUNK, :].rearrange(
                    "i (r s) e -> r i (s e)", s=RUN
                ),
                in_=to_store[:].rearrange("r i s e -> r i (s e)"),
            )

        def turn_and_store(chunk, copy=nc.scalar.copy):
            for n in range(N_QKV):
                turn(chunk, n)
                store(chunk, n, copy)

        def spread(column, scale=1.0):
            turned = psum_turned.tile([P, P], F32)
            nc.tensor.transpose(turned[:], column.to_broadcast([P, P]), identity[:])
            row = rows_pool.tile([P, P], F32)
            nc.scalar.activation(out=row[:], in_=turned[:], func=ACT.Copy, scale=scale)
            return row

        def multiply_direct(chunk, n):
            b, q = divmod(chunk, CHUNKS)
            a_codes, a_scales = code_tiles[b]
            h = psum_products.tile([P, RUN, P], F32)
            for s in range(RUN):
                for c in range(PASSES):
                    nc.tensor.matmul_mx(
                        out=h[:, s, :],
                        lhsT=a_codes[:, q, c, s * P : (s + 1) * P].bitcast(FP8X4),
                        lhsT_scale=a_scales[:, q, c, s * P : (s + 1) * P],
                        rhs=w_codes[:, n, c, :].bitcast(FP8X4),
                        rhs_scale=w_scales[:, n, c, :],
                        start=(c == 0),
                        stop=(c == PASSES - 1),
                    )
            return h

        def store_direct(chunk, n, h, row):
            b, q = divmod(chunk, CHUNKS)
            to_store = store_pool.tile([P, HEADS, RUN, HEAD_DIM], F32)
            nc.vector.tensor_mul(
                out=to_store[:].rearrange("r i s e -> r s i e"),
                in0=h[:].rearrange("r s (i e) -> r s i e", i=HEADS),
                in1=row[:]
                .rearrange("r (i e) -> r i e", i=HEADS)
                .unsqueeze(1)
                .to_broadcast([P, RUN, HEADS, HEAD_DIM]),
            )
            nc.sync.dma_start(
                out=out[n, b, :, q * CHUNK : (q + 1) * CHUNK, :].rearrange(
                    "i (r s) e -> r i (s e)", s=RUN
                ),
                in_=to_store[:].rearrange("r i s e -> r i (s e)"),
            )

        w_raw = const.tile([P, N_QKV, HEADS, PASSES, PACK, HEAD_DIM], BF16)

        def load_weights(n):
            nc.sync.dma_start(
                out=w_raw[:, n],
                in_=qkv[n].rearrange("i (c p j) e -> p i c j e", c=PASSES, p=P, j=PACK),
            )

        load_first_half()
        load_weights(0)
        load_half(1)
        for n in range(1, N_QKV):
            load_weights(n)
        for half in range(2, LOADS_AHEAD):
            load_half(half)
        gain_bf16 = const.tile([P, 1], BF16)
        nc.sync.dma_start(out=gain_bf16[:], in_=norm_w.partition_broadcast(P))

        eps = const.tile([P, 1], F32)
        nc.vector.memset(eps[:], EPS)
        table_warmer = const.tile([P, 1], F32)
        nc.scalar.activation(out=table_warmer[:], in_=eps[:], func=ACT.Abs_reciprocal_sqrt)
        identity = const.tile([P, P], F32)
        make_identity(nc, identity[:])
        gain = const.tile([P, 1], F32)

        w_grouped = const.tile([P, N_QKV, PASSES, HEADS, HEAD_DIM, PACK], BF16, align_bytes=64)
        w_codes = const.tile([P, N_QKV, PASSES, P], U32, align_bytes=64)
        w_scales = const.tile([P, N_QKV, PASSES, P], U8, align_bytes=64)
        for n in range(N_QKV):
            for c in range(PASSES):
                nc.scalar.copy(
                    out=w_grouped[:, n, c],
                    in_=w_raw[:, n, :, c].rearrange("p i j e -> p i e j"),
                )

        def quantise_weights():
            for n in range(N_QKV):
                nc.vector.quantize_mx(
                    out=w_codes[:, n].rearrange("p c m -> p (c m)").bitcast(FP8X4),
                    scales=w_scales[:, n].rearrange("p c m -> p (c m)"),
                    in_=w_grouped[:, n].rearrange("p c i e j -> p (c i e j)"),
                )

        for half in range(HELP_AHEAD):
            if scalar_helps(half):
                regroup_half_on_scalar(half)

        for step in range(ALL_CHUNKS):
            for half in range(PASSES * step, PASSES * (step + 1)):
                if half + HELP_AHEAD not in LATE and scalar_helps(half + HELP_AHEAD):
                    regroup_half_on_scalar(half + HELP_AHEAD)
                k, rest = divmod(half - LATE_FROM, LATE_EVERY)
                if rest == 0 and 0 <= k < len(LATE):
                    regroup_half_on_scalar(LATE[k])
                    if k + LATE_LOADS < len(LATE):
                        load_half(LATE[k + LATE_LOADS])
                if half == 1:
                    for k in range(LATE_LOADS):
                        load_half(LATE[k])
                begin_leaky_relu(half)
                if half + LOADS_AHEAD < HALVES and half + LOADS_AHEAD not in LATE:
                    load_half(half + LOADS_AHEAD)
                if half >= 1:
                    quantise_half(half - 1)
                end_leaky_relu(half)
                if half == PASSES:
                    quantise_weights()
            if step == ALL_CHUNKS - 1:
                quantise_half(HALVES - 1)

            if step >= 1:
                sum_squares_of_chunk(step - 1)
                if step == CHUNKS:
                    nc.scalar.copy(out=gain[:], in_=gain_bf16[:])
                if step % CHUNKS == 0:
                    norm_factor_of_batch(step // CHUNKS - 1)
            if SCALE_LAG <= step < ALL_CHUNKS - 1:
                chunk = step - SCALE_LAG
                for n in range(N_QKV):
                    scale(chunk, n, project(chunk, n), scale_on_scalar(chunk // CHUNKS, n))
            if STORE_LAG <= step < ALL_CHUNKS - 1:
                turn_and_store(step - STORE_LAG)

        b, last = BATCH - 1, ALL_CHUNKS - 1
        first = last - CHUNKS + 1
        mean_before = stats_pool.tile([P, N_QKV], F32)
        addends = stats_pool.tile([P, N_QKV, CHUNKS - 1], F32)
        mean_and_eps = stats_pool.tile([P, N_QKV], F32)
        inverse_rms = [stats_pool.tile([P, 1], F32, name="inverse_rms_%d" % n) for n in range(N_QKV)]
        products = {}
        rows = {}

        def mean_without_last_chunk():
            for n in range(N_QKV):
                nc.scalar.activation(
                    out=addends[:, n, :],
                    in_=sum_tiles[b][:, n, 0 : CHUNKS - 1],
                    func=ACT.Copy,
                    scale=1.0 / SEQ,
                    accum_out=mean_before[:, n : n + 1],
                )
            nc.scalar.activation(
                out=mean_and_eps[:], in_=mean_before[:], func=ACT.Identity, bias=eps[:, 0:1]
            )

        def scale_by_parts(n):
            return lambda to, h: nc.vector.tensor_scalar(
                out=to,
                in0=h,
                scalar1=inverse_rms[n][:, 0:1],
                scalar2=gain[:, 0:1],
                op0=ALU.mult,
                op1=ALU.mult,
            )

        def form(chunk, *ns):
            for n in ns:
                make = multiply_direct if chunk in DIRECT else project
                products[(chunk, n)] = make(chunk, n)

        def scale_late(chunk, *ns):
            for n in ns:
                how = scale_by_parts(n) if chunk >= first else scale_on_vector(b - 1, n)
                scale(chunk, n, products[(chunk, n)], how)

        def turn_all(chunk, *ns):
            for n in ns:
                turn(chunk, n)

        def store_all(chunk, *ns, copy=nc.scalar.copy):
            for n in ns:
                store(chunk, n, copy)

        def square(n):
            sum_squares(last, n, products[(last, n)])

        def root(n):
            nc.scalar.activation(
                out=inverse_rms[n][:],
                in_=sum_tiles[b][:, n, CHUNKS - 1 : CHUNKS],
                func=ACT.Abs_reciprocal_sqrt,
                scale=1.0 / SEQ,
                bias=mean_and_eps[:, n : n + 1],
            )

        def spread_row(n):
            rows[n] = spread(inverse_rms[n][:], gain[:, 0:1])

        def direct(n):
            for chunk in DIRECT:
                store_direct(chunk, n, products[(chunk, n)], rows[n])

        everything = range(N_QKV)
        form(first - 1, 0, 1)
        turn_all(first - 2, *everything)
        scale_late(first - 1, 0, 1)
        store_all(first - 2, *everything, copy=nc.vector.tensor_copy)
        mean_without_last_chunk()
        form(last, *everything)
        form(first - 1, 2)
        scale_late(first - 1, 2)
        square(0)
        root(0)
        square(1)
        root(1)
        turn_all(first - 1, 0)
        form(first, 0)
        store_all(first - 1, 0)
        scale_late(last, 0)
        square(2)
        spread_row(0)
        root(2)
        turn_all(first - 1, 1, 2)
        scale_late(last, 1, 2)
        store_all(first - 1, 1, 2)
        turn_all(last, 0)
        spread_row(1)
        store_all(last, 0)
        form(last - 1, 0)
        form(first + 1, 0)
        turn_all(last, 1)
        spread_row(2)
        store_all(last, 1)
        direct(0)
        scale_late(last - 1, 0)
        form(first + 1, 1)
        form(first, 1)
        turn_all(last, 2)
        turn_all(last - 1, 0)
        store_all(last, 2)
        store_all(last - 1, 0)
        direct(1)
        form(last - 1, 1)
        form(first + 1, 2)
        form(first, 2)
        form(last - 1, 2)
        scale_late(last - 1, 1)
        turn_all(last - 1, 1)
        direct(2)
        scale_late(last - 1, 2)
        turn_all(last - 1, 2)
        store_all(last - 1, 1, 2)
